import numpy as np
import ml_dtypes


def mxq(x, axis, fmt="e4m3"):
    dtype, down = {"e4m3": (ml_dtypes.float8_e4m3fn, 7), "e5m2": (ml_dtypes.float8_e5m2, 14)}[fmt]
    v = np.moveaxis(np.asarray(x, np.float32).astype(ml_dtypes.bfloat16).astype(np.float64), axis, -1)
    blocks = v.reshape(v.shape[:-1] + (-1, 32))
    amax = np.abs(blocks).max(-1, keepdims=True)
    byte = np.maximum(np.where(amax > 0, np.frexp(amax)[1] - 1 + 127, 0) - down, 1)
    scale = np.exp2(byte - 127.0)
    codes = (blocks / scale).astype(np.float32).astype(dtype).astype(np.float64)
    return np.moveaxis((codes * scale).reshape(v.shape), -1, axis)


WIDE = False


def mx_kscale(k):
    if not WIDE:
        return np.ones(k)
    levels = np.array([10, -10, 5, -5, 0])
    if k % 512:
        return np.exp2(np.random.permutation(np.resize(levels, k // 32))).repeat(32)
    a = np.empty((k // 512, 16))
    for p in range(k // 512):
        a[p, :8] = np.random.permutation(np.resize(levels, 8))
        for g in range(8):
            far = levels[np.abs(levels - a[p, g]) >= 10]
            a[p, g + 8] = far[np.random.randint(len(far))]
    return np.exp2(a.ravel()).repeat(32)


BF16 = ml_dtypes.bfloat16


def bf(x):
    return np.asarray(x, np.float32).astype(BF16)


def f64(x):
    return np.asarray(x).astype(np.float64)


B, T, D, DI = 4, 1024, 512, 512
ROPE_BASE = 10000.0


def rotate_half(v):
    h = v.shape[-1] // 2
    return np.concatenate([-v[..., h:], v[..., :h]], axis=-1)


def justnorm(v):
    return v / np.sqrt((v * v).sum(-1, keepdims=True))


def setup_inputs():
    s = mx_kscale(D)
    x = np.random.standard_normal((B, T, D)) * np.exp(0.5 * np.random.standard_normal((B, T, 1)))
    w = justnorm(np.random.uniform(-1.0, 1.0, (2 * DI, D)))
    inv_freq = 1.0 / ROPE_BASE ** (np.arange(0, DI, 2) / DI)
    pos = np.random.randint(0, T) + np.arange(T)
    freqs = pos[:, None] * inv_freq[None, :]
    emb = np.concatenate([freqs, freqs], axis=-1)
    return {"input_vecs": bf(x * s), "qk_w": bf(w / s),
            "sqk": bf(3.0 * (1.0 + 0.2 * np.random.standard_normal(DI)) / np.sqrt(D)),
            "cos": bf(np.cos(emb)), "sin": bf(np.sin(emb))}


def reference(input_vecs, qk_w, sqk, cos, sin):
    qk = mxq(f64(input_vecs), 2, "e4m3") @ mxq(f64(qk_w), 1, "e4m3").T
    q, k = np.split(qk, 2, axis=-1)
    c, sn = f64(cos), f64(sin)
    q = q * c + rotate_half(q) * sn
    k = k * c + rotate_half(k) * sn
    sqk_eff = f64(sqk) * np.sqrt(D)
    return justnorm(q) * sqk_eff, justnorm(k) * sqk_eff

@@ -1,0 +1,318 @@
+from contextlib import ExitStack
+
+import concourse.mybir as mybir
+from concourse.masks import make_identity
+
+F32 = mybir.dt.float32
+BF16 = mybir.dt.bfloat16
+U32 = mybir.dt.uint32
+U8 = mybir.dt.uint8
+FP8X4 = mybir.dt.float8_e4m3fn_x4
+ACT = mybir.ActivationFunctionType
+ALU = mybir.AluOpType
+
+P = 128
+B, T, D, DI = 4, 1024, 512, 512
+NT = T // P
+NPAIR = NT // 2
+NJ = DI // P
+GT = 2 * P
+NS = B * NPAIR
+NG = 2 * NS
+DUP = 3
+XE_ON_S = (1,)
+SPIN_FIRST = 6
+FLOPS = 2 * B * T * D * 2 * DI
+
+
+def tile_attentionhead_pa_t_kernel(tc, input_vecs, qk_w, sqk, cos, sin, out_0, out_1):
+    nc = tc.nc
+    x_v = input_vecs.rearrange("b (p n) k -> b p n k", n=NT)
+    w_v = qk_w.rearrange("(r p) k -> p r k", p=P)
+    cos_v = cos.rearrange("(p n) c -> p n c", n=NT)
+    sin_v = sin.rearrange("(p n) c -> p n c", n=NT)
+    o_v = [o.rearrange("b (p n) c -> b p n c", n=NT) for o in (out_0, out_1)]
+
+    with ExitStack() as ctx:
+        const = ctx.enter_context(tc.tile_pool(name="const", bufs=1))
+        stage = ctx.enter_context(tc.tile_pool(name="stage", bufs=3))
+        prods = ctx.enter_context(tc.tile_pool(name="prods", bufs=6))
+        outs = ctx.enter_context(tc.tile_pool(name="outs", bufs=4))
+        small = ctx.enter_context(tc.tile_pool(name="small", bufs=4))
+        psum_mx = ctx.enter_context(tc.psum_pool(name="psum_mx", bufs=3))
+        psum_tp = ctx.enter_context(tc.psum_pool(name="psum_tp", bufs=5))
+        ctx.enter_context(tc.manual_schedule())
+
+        ident_f = const.tile([P, P], F32, name="ident_f")
+        make_identity(nc, ident_f[:])
+        ident_b = const.tile([P, P], BF16, name="ident_b")
+        make_identity(nc, ident_b[:])
+        one = const.tile([P, 1], F32, name="one")
+        nc.vector.memset(one[:], 1.0)
+        warm = const.tile([P, 1], F32, name="warm")
+        nc.scalar.activation(out=warm[:], in_=one[:], func=ACT.Abs_reciprocal_sqrt)
+        zl = const.tile([P, P], BF16, name="zl")
+        nc.vector.memset(zl[:], 0.0)
+        zr = const.tile([P, 2 * GT], BF16, name="zr")
+        nc.vector.memset(zr[:], 0.0)
+        dm = psum_mx.tile([P, 2 * GT], F32, tag="mx", name="dm")
+
+        def spin(n):
+            for rep in range(n):
+                nc.tensor.matmul(out=dm[:], lhsT=zl[:], rhs=zr[:], start=True, stop=True)
+
+        spin(SPIN_FIRST)
+
+        xr = [const.tile([P, NT, D], BF16, name="xr%d" % b) for b in range(B)]
+        wr = const.tile([P, 2 * NJ, D], BF16, name="wr")
+        cr = const.tile([P, NT, DI], BF16, name="cr")
+        sr = const.tile([P, NT, DI], BF16, name="sr")
+        gb = const.tile([P, DI], BF16, name="gb")
+        xc = const.tile([P, B * T], U32, name="xc", align_bytes=64)
+        xs = const.tile([P, B * T], U8, name="xs", align_bytes=64)
+        wc = const.tile([P, 2 * DI], U32, name="wc", align_bytes=64)
+        ws = const.tile([P, 2 * DI], U8, name="ws", align_bytes=64)
+        tabs = const.tile([P, 2, NJ, NPAIR, GT], BF16, name="tabs")
+
+        nc.sync.dma_start(out=wr[:, 0:2, :], in_=w_v[:, 0:2, :])
+        nc.sync.dma_start(out=wr[:, 2:NJ, :], in_=w_v[:, 2:NJ, :])
+        nc.sync.dma_start(out=xr[0][:, 0:2, :], in_=x_v[0][:, 0:2, :])
+        nc.sync.dma_start(out=wr[:, NJ : 2 * NJ, :], in_=w_v[:, NJ : 2 * NJ, :])
+        for lo, hi in ((0, 2), (2, 4), (4, 8)):
+            if lo > 0:
+                nc.sync.dma_start(out=xr[0][:, lo:hi, :], in_=x_v[0][:, lo:hi, :])
+            nc.sync.dma_start(out=cr[:, lo:hi, :], in_=cos_v[:, lo:hi, :])
+            nc.sync.dma_start(out=sr[:, lo:hi, :], in_=sin_v[:, lo:hi, :])
+        nc.sync.dma_start(out=gb[:], in_=sqk.partition_broadcast(P))
+        for b in range(1, B):
+            nc.sync.dma_start(out=xr[b][:], in_=x_v[b])
+
+        grouped = {}
+        word_banks = {}
+        banks = {}
+        prod_tiles = {}
+        r_banks = {}
+        norm_tiles = {}
+
+        def rows_tp(key, rows):
+            pts = []
+            for m in range(len(rows) // 2):
+                pt = psum_tp.tile([P, 2, 2, P], F32, tag="tp", name="pt")
+                pts.append(pt)
+                for i in range(2):
+                    words = rows[2 * m + i].bitcast(F32)
+                    for u in range(2):
+                        nc.tensor.transpose(pt[:, i, u, :], words[:, u : 2 * P : 2], ident_f[:])
+            word_banks[key] = pts
+
+        def rows_ev(key, on_scalar):
+            pts = word_banks[key]
+            g_t = stage.tile([P, len(pts) * 2 * P * 4], BF16, tag="g%d" % len(pts), name="g_t", align_bytes=64)
+            grouped[key] = g_t
+            gw = g_t[:].bitcast(F32).rearrange("p (m i r u) -> p m i r u", i=2, r=P, u=2)
+            for m in range(len(pts)):
+                src = pts[m][:].rearrange("p i u r -> p i r u")
+                if on_scalar[m]:
+                    nc.scalar.copy(out=gw[:, m], in_=src)
+                else:
+                    nc.vector.tensor_copy(out=gw[:, m], in_=src)
+
+        def w_tp(h):
+            rows_tp(("w", h), [wr[:, h * NJ + j, :] for j in range(NJ)])
+
+        def w_q(h):
+            cols = slice(h * DI, (h + 1) * DI)
+            nc.vector.quantize_mx(out=wc[:, cols].bitcast(FP8X4), scales=ws[:, cols], in_=grouped[("w", h)][:])
+
+        def x_tp(s):
+            b, q = divmod(s, NPAIR)
+            rows_tp(("x", s), [xr[b][:, 2 * q + i, :] for i in range(2)])
+
+        def x_q(s):
+            cols = slice(s * GT, (s + 1) * GT)
+            nc.vector.quantize_mx(out=xc[:, cols].bitcast(FP8X4), scales=xs[:, cols], in_=grouped[("x", s)][:])
+
+        def tab(q, is_sin):
+            raw = sr if is_sin else cr
+            ptb = psum_tp.tile([P, NJ, GT], BF16, tag="tp", name="ptb")
+            for j in range(NJ):
+                for i in range(2):
+                    nc.tensor.transpose(
+                        ptb[:, j, i * P : (i + 1) * P], raw[:, 2 * q + i, j * P : (j + 1) * P], ident_b[:]
+                    )
+            if is_sin:
+                nc.scalar.copy(out=tabs[:, 1, 0:2, q, :], in_=ptb[:, 2:4, :])
+                nc.scalar.mul(out=tabs[:, 1, 2:4, q, :], in_=ptb[:, 0:2, :], mul=-1.0)
+            else:
+                nc.scalar.copy(out=tabs[:, 0, :, q, :], in_=ptb[:])
+
+        def mx(g, dup):
+            s, h = divmod(g, 2)
+            tok = slice(s * GT, (s + 1) * GT)
+            banks[g] = []
+            for pr in range(2):
+                x2 = psum_mx.tile([P, 2, GT], F32, tag="mx", name="x2")
+                banks[g].append(x2)
+                for t2 in range(2):
+                    c0 = h * DI + (pr + 2 * t2) * P
+                    for rep in range(2 if 2 * pr + t2 < dup else 1):
+                        nc.tensor.matmul_mx(
+                            out=x2[:, t2, :],
+                            lhsT=wc[:, c0 : c0 + P].bitcast(FP8X4),
+                            lhsT_scale=ws[:, c0 : c0 + P],
+                            rhs=xc[:, tok].bitcast(FP8X4),
+                            rhs_scale=xs[:, tok],
+                            start=True,
+                            stop=True,
+                        )
+
+        def prod(g, pr):
+            q = (g // 2) % NPAIR
+            ab = prods.tile([P, 2, 2, GT], F32, tag="ab", name="ab")
+            prod_tiles[(g, pr)] = ab
+            nc.vector.tensor_tensor(
+                out=ab[:],
+                in0=banks[g][pr][:].unsqueeze(1).to_broadcast([P, 2, 2, GT]),
+                in1=tabs[:, :, slice(pr, NJ, 2), q, :],
+                op=ALU.mult,
+            )
+
+        def add_t(g):
+            r_banks[g] = []
+            for i in range(2):
+                rb = psum_tp.tile([P, DI], F32, tag="tp", name="rb")
+                r_banks[g].append(rb)
+                ts = slice(i * P, (i + 1) * P)
+                for pr in range(2):
+                    ab = prod_tiles[(g, pr)]
+                    for t2 in range(2):
+                        j = pr + 2 * t2
+                        cs = slice(j * P, (j + 1) * P)
+                        nc.tensor.matmul(
+                            out=rb[:, cs],
+                            lhsT=ab[:, 0, t2, ts],
+                            rhs=ident_f[:],
+                            is_transpose=True,
+                            start=True,
+                            stop=False,
+                        )
+                        nc.tensor.matmul(
+                            out=rb[:, cs],
+                            lhsT=ab[:, 1, 1 - t2, ts],
+                            rhs=ident_f[:],
+                            is_transpose=True,
+                            start=False,
+                            stop=True,
+                        )
+
+        def sum_squares(g, i):
+            if i == 0:
+                ssq = small.tile([P, 2], F32, tag="ssq", name="ssq")
+                rho = small.tile([P, 2], F32, tag="rho", name="rho")
+                ot = outs.tile([P, 2, DI], F32, tag="ot", name="ot")
+                norm_tiles[g] = (ssq, rho, ot)
+            junk = stage.tile([P, DI], BF16, tag="junk", name="junk")
+            nc.scalar.activation(
+                out=junk[:], in_=r_banks[g][i][:], func=ACT.Square, accum_out=norm_tiles[g][0][:, i : i + 1]
+            )
+
+        def inv_norm(g, i):
+            ssq, rho, ot = norm_tiles[g]
+            col = slice(i, i + 1)
+            nc.scalar.activation(out=rho[:, col], in_=ssq[:, col], func=ACT.Abs_reciprocal_sqrt, scale=1.0 / D)
+
+        def scale_out(g, i):
+            ssq, rho, ot = norm_tiles[g]
+            nc.scalar.activation(out=ot[:, i, :], in_=r_banks[g][i][:], func=ACT.Copy, scale=rho[:, i : i + 1])
+
+        def gain_store(g):
+            s, h = divmod(g, 2)
+            b, q = divmod(s, NPAIR)
+            ot = norm_tiles[g][2]
+            nc.gpsimd.tensor_tensor(
+                out=ot[:], in0=ot[:], in1=gb[:].unsqueeze(1).to_broadcast([P, 2, DI]), op=ALU.mult
+            )
+            nc.sync.dma_start(out=o_v[h][b][:, 2 * q : 2 * q + 2, :], in_=ot[:])
+
+        def gain_store_unit(g, i):
+            s, h = divmod(g, 2)
+            b, q = divmod(s, NPAIR)
+            ot = norm_tiles[g][2]
+            nc.gpsimd.tensor_tensor(out=ot[:, i, :], in0=ot[:, i, :], in1=gb[:], op=ALU.mult)
+            nc.sync.dma_start(out=o_v[h][b][:, 2 * q + i, :], in_=ot[:, i, :])
+
+        def last_unit(g, i):
+            s, h = divmod(g, 2)
+            b, q = divmod(s, NPAIR)
+            ssq, rho, ot = norm_tiles[g]
+            nc.vector.scalar_tensor_tensor(
+                out=ot[:, i, :],
+                in0=r_banks[g][i][:],
+                scalar=rho[:, i : i + 1],
+                in1=gb[:],
+                op0=ALU.mult,
+                op1=ALU.mult,
+            )
+            nc.sync.dma_start(out=o_v[h][b][:, 2 * q + i, :], in_=ot[:, i, :])
+
+        def finish(g):
+            last = g == NG - 1
+            sum_squares(g, 0)
+            if last:
+                last_unit(g - 1, 1)
+            elif g >= 1:
+                scale_out(g - 1, 1)
+                gain_store(g - 1)
+            inv_norm(g, 0)
+            if last:
+                last_unit(g, 0)
+            sum_squares(g, 1)
+            if not last:
+                scale_out(g, 0)
+            if g == NG - 2:
+                gain_store_unit(g, 0)
+            inv_norm(g, 1)
+            if last:
+                last_unit(g, 1)
+
+        w_tp(0)
+        spin(1)
+        rows_ev(("w", 0), (False, True))
+        x_tp(0)
+        rows_ev(("x", 0), (False,))
+        w_q(0)
+        x_q(0)
+        w_tp(1)
+        spin(1)
+        rows_ev(("w", 1), (True, False))
+        w_q(1)
+        tab(0, False)
+        spin(1)
+        tab(0, True)
+        spin(1)
+        mx(0, 0)
+        x_tp(1)
+        rows_ev(("x", 1), (True,))
+
+        tab_at = {0: ((1, False), (1, True)), 1: ((2, False),), 2: ((2, True),), 3: ((3, False),), 4: ((3, True),)}
+        for it in range(NG + 1):
+            s_new = (it + 3) // 2 if it % 2 == 1 and (it + 3) // 2 < NS else None
+            if it >= 1:
+                add_t(it - 1)
+            if s_new is not None:
+                x_tp(s_new)
+            if it < NG:
+                prod(it, 0)
+                prod(it, 1)
+            if s_new is not None and s_new not in XE_ON_S:
+                rows_ev(("x", s_new), (False,))
+            if it % 2 == 0 and (it + 2) // 2 < NS:
+                x_q((it + 2) // 2)
+            if it + 1 < NG:
+                mx(it + 1, DUP)
+            if it >= 1:
+                finish(it - 1)
+            if s_new is not None and s_new in XE_ON_S:
+                rows_ev(("x", s_new), (True,))
+            for q, is_sin in tab_at.get(it, ()):
+                tab(q, is_sin)

@@ -19,9 +19,10 @@ NJ = DI // P
 GT = 2 * P
 NS = B * NPAIR
 NG = 2 * NS
-DUP = 3
+DUP = 0
+PLAIN = (2, 5)
 XE_ON_S = (1,)
-SPIN_FIRST = 6
+SPIN_FIRST = 4
 FLOPS = 2 * B * T * D * 2 * DI
 
 
@@ -192,7 +193,7 @@ def tile_attentionhead_pa_t_kernel(tc, input_vecs, qk_w, sqk, cos, sin, out_0, o
                             out=rb[:, cs],
                             lhsT=ab[:, 0, t2, ts],
                             rhs=ident_f[:],
-                            is_transpose=True,
+                            is_transpose=4 * i + 2 * pr + t2 not in PLAIN,
                             start=True,
                             stop=False,
                         )

@@ -21,7 +21,6 @@ NS = B * NPAIR
 NG = 2 * NS
 DUP = 0
 PLAIN = (2, 5)
-XE_ON_S = (1,)
 SPIN_FIRST = 4
 FLOPS = 2 * B * T * D * 2 * DI
 
@@ -226,12 +225,19 @@ def tile_attentionhead_pa_t_kernel(tc, input_vecs, qk_w, sqk, cos, sin, out_0, o
             ssq, rho, ot = norm_tiles[g]
             nc.scalar.activation(out=ot[:, i, :], in_=r_banks[g][i][:], func=ACT.Copy, scale=rho[:, i : i + 1])
 
+        def on_v(g):
+            return g % 2 == 1
+
         def gain_store(g):
             s, h = divmod(g, 2)
             b, q = divmod(s, NPAIR)
             ot = norm_tiles[g][2]
+            n = 1 if on_v(g) else 2
             nc.gpsimd.tensor_tensor(
-                out=ot[:], in0=ot[:], in1=gb[:].unsqueeze(1).to_broadcast([P, 2, DI]), op=ALU.mult
+                out=ot[:, 0:n, :],
+                in0=ot[:, 0:n, :],
+                in1=gb[:].unsqueeze(1).to_broadcast([P, n, DI]),
+                op=ALU.mult,
             )
             nc.sync.dma_start(out=o_v[h][b][:, 2 * q : 2 * q + 2, :], in_=ot[:])
 
@@ -242,9 +248,7 @@ def tile_attentionhead_pa_t_kernel(tc, input_vecs, qk_w, sqk, cos, sin, out_0, o
             nc.gpsimd.tensor_tensor(out=ot[:, i, :], in0=ot[:, i, :], in1=gb[:], op=ALU.mult)
             nc.sync.dma_start(out=o_v[h][b][:, 2 * q + i, :], in_=ot[:, i, :])
 
-        def last_unit(g, i):
-            s, h = divmod(g, 2)
-            b, q = divmod(s, NPAIR)
+        def norm_gain_on_v(g, i):
             ssq, rho, ot = norm_tiles[g]
             nc.vector.scalar_tensor_tensor(
                 out=ot[:, i, :],
@@ -254,6 +258,12 @@ def tile_attentionhead_pa_t_kernel(tc, input_vecs, qk_w, sqk, cos, sin, out_0, o
                 op0=ALU.mult,
                 op1=ALU.mult,
             )
+
+        def last_unit(g, i):
+            s, h = divmod(g, 2)
+            b, q = divmod(s, NPAIR)
+            ot = norm_tiles[g][2]
+            norm_gain_on_v(g, i)
             nc.sync.dma_start(out=o_v[h][b][:, 2 * q + i, :], in_=ot[:, i, :])
 
         def finish(g):
@@ -262,7 +272,8 @@ def tile_attentionhead_pa_t_kernel(tc, input_vecs, qk_w, sqk, cos, sin, out_0, o
             if last:
                 last_unit(g - 1, 1)
             elif g >= 1:
-                scale_out(g - 1, 1)
+                if not on_v(g - 1):
+                    scale_out(g - 1, 1)
                 gain_store(g - 1)
             inv_norm(g, 0)
             if last:
@@ -304,16 +315,16 @@ def tile_attentionhead_pa_t_kernel(tc, input_vecs, qk_w, sqk, cos, sin, out_0, o
                 x_tp(s_new)
             if it < NG:
                 prod(it, 0)
+                if it >= 2 and on_v(it - 2):
+                    norm_gain_on_v(it - 2, 1)
                 prod(it, 1)
-            if s_new is not None and s_new not in XE_ON_S:
-                rows_ev(("x", s_new), (False,))
             if it % 2 == 0 and (it + 2) // 2 < NS:
                 x_q((it + 2) // 2)
             if it + 1 < NG:
                 mx(it + 1, DUP)
             if it >= 1:
                 finish(it - 1)
-            if s_new is not None and s_new in XE_ON_S:
+            if s_new is not None:
                 rows_ev(("x", s_new), (True,))
             for q, is_sin in tab_at.get(it, ()):
                 tab(q, is_sin)

@@ -1,3 +1,4 @@
+import math
 from contextlib import ExitStack
 
 import concourse.mybir as mybir
@@ -13,16 +14,34 @@ ALU = mybir.AluOpType
 
 P = 128
 B, T, D, DI = 4, 1024, 512, 512
+H = DI // 2
 NT = T // P
 NPAIR = NT // 2
 NJ = DI // P
 GT = 2 * P
 NS = B * NPAIR
-NG = 2 * NS
+TMQ = ()
+NC = NPAIR - len(TMQ)
 DUP = 0
 PLAIN = (2, 5)
-SPIN_FIRST = 4
+ONV = 8
+INV = "s"
+TLEAD = 2
+XEV = True
+G_SCALE = False
+MX_FIRST = False
+BMX = 3
+BR = 5
+BPT = 0
+LEADT = 3
+LEADQ = 2
+SPIN_FIRST = 3
 FLOPS = 2 * B * T * D * 2 * DI
+
+BORDER = ((0, 0), (0, 1), (1, 0), (3, 0), (1, 1), (2, 0), (3, 1), (2, 1))
+QMAJOR = True
+ORDER = [(b * NPAIR + q, h) for q in range(NPAIR) for b in range(B) for h in range(2)] if QMAJOR else [(batch * NPAIR + pair, half) for batch in range(B) for pair, half in (BORDER if TMQ else [(a, c) for a in range(4) for c in range(2)])]
+NG = len(ORDER)
 
 
 def tile_attentionhead_pa_t_kernel(tc, input_vecs, qk_w, sqk, cos, sin, out_0, out_1):
@@ -37,20 +56,23 @@ def tile_attentionhead_pa_t_kernel(tc, input_vecs, qk_w, sqk, cos, sin, out_0, o
         const = ctx.enter_context(tc.tile_pool(name="const", bufs=1))
         stage = ctx.enter_context(tc.tile_pool(name="stage", bufs=3))
         prods = ctx.enter_context(tc.tile_pool(name="prods", bufs=6))
-        outs = ctx.enter_context(tc.tile_pool(name="outs", bufs=4))
-        small = ctx.enter_context(tc.tile_pool(name="small", bufs=4))
-        psum_mx = ctx.enter_context(tc.psum_pool(name="psum_mx", bufs=3))
-        psum_tp = ctx.enter_context(tc.psum_pool(name="psum_tp", bufs=5))
+        outs = ctx.enter_context(tc.tile_pool(name="outs", bufs=7))
+        small = ctx.enter_context(tc.tile_pool(name="small", bufs=8))
+        psum_mx = ctx.enter_context(tc.psum_pool(name="psum_mx", bufs=BMX))
+        psum_tp = ctx.enter_context(tc.psum_pool(name="psum_tp", bufs=BR))
+        psum_pt = ctx.enter_context(tc.psum_pool(name="psum_pt", bufs=BPT)) if BPT else psum_tp
         ctx.enter_context(tc.manual_schedule())
 
         ident_f = const.tile([P, P], F32, name="ident_f")
         make_identity(nc, ident_f[:])
         ident_b = const.tile([P, P], BF16, name="ident_b")
         make_identity(nc, ident_b[:])
+        mhalf = const.tile([P, 2], F32, name="mhalf")
+        nc.vector.memset(mhalf[:], -0.5)
         one = const.tile([P, 1], F32, name="one")
         nc.vector.memset(one[:], 1.0)
         warm = const.tile([P, 1], F32, name="warm")
-        nc.scalar.activation(out=warm[:], in_=one[:], func=ACT.Abs_reciprocal_sqrt)
+        nc.scalar.activation(out=warm[:], in_=one[:], func=ACT.Square if INV == "g" else ACT.Abs_reciprocal_sqrt)
         zl = const.tile([P, P], BF16, name="zl")
         nc.vector.memset(zl[:], 0.0)
         zr = const.tile([P, 2 * GT], BF16, name="zr")
@@ -67,37 +89,46 @@ def tile_attentionhead_pa_t_kernel(tc, input_vecs, qk_w, sqk, cos, sin, out_0, o
         wr = const.tile([P, 2 * NJ, D], BF16, name="wr")
         cr = const.tile([P, NT, DI], BF16, name="cr")
         sr = const.tile([P, NT, DI], BF16, name="sr")
-        gb = const.tile([P, DI], BF16, name="gb")
+        gb_raw = const.tile([P, DI], BF16, name="gb_raw")
+        gb = const.tile([P, DI], F32, name="gb") if INV == "g" else gb_raw
+        sneg = const.tile([P, 2, H], BF16, name="sneg")
         xc = const.tile([P, B * T], U32, name="xc", align_bytes=64)
         xs = const.tile([P, B * T], U8, name="xs", align_bytes=64)
         wc = const.tile([P, 2 * DI], U32, name="wc", align_bytes=64)
         ws = const.tile([P, 2 * DI], U8, name="ws", align_bytes=64)
-        tabs = const.tile([P, 2, NJ, NPAIR, GT], BF16, name="tabs")
+        tabs = const.tile([P, 2, NJ, NC, GT], BF16, name="tabs")
 
         nc.sync.dma_start(out=wr[:, 0:2, :], in_=w_v[:, 0:2, :])
         nc.sync.dma_start(out=wr[:, 2:NJ, :], in_=w_v[:, 2:NJ, :])
-        nc.sync.dma_start(out=xr[0][:, 0:2, :], in_=x_v[0][:, 0:2, :])
-        nc.sync.dma_start(out=wr[:, NJ : 2 * NJ, :], in_=w_v[:, NJ : 2 * NJ, :])
-        for lo, hi in ((0, 2), (2, 4), (4, 8)):
-            if lo > 0:
-                nc.sync.dma_start(out=xr[0][:, lo:hi, :], in_=x_v[0][:, lo:hi, :])
-            nc.sync.dma_start(out=cr[:, lo:hi, :], in_=cos_v[:, lo:hi, :])
-            nc.sync.dma_start(out=sr[:, lo:hi, :], in_=sin_v[:, lo:hi, :])
-        nc.sync.dma_start(out=gb[:], in_=sqk.partition_broadcast(P))
-        for b in range(1, B):
-            nc.sync.dma_start(out=xr[b][:], in_=x_v[b])
+        x_order = []
+        for s, h in ORDER:
+            if s not in x_order:
+                x_order.append(s)
+        q_seen = []
+        for n, s in enumerate(x_order):
+            b, q = divmod(s, NPAIR)
+            pair = slice(2 * q, 2 * q + 2)
+            nc.sync.dma_start(out=xr[b][:, pair, :], in_=x_v[b][:, pair, :])
+            if q not in q_seen:
+                q_seen.append(q)
+                nc.sync.dma_start(out=cr[:, pair, :], in_=cos_v[:, pair, :])
+                nc.sync.dma_start(out=sr[:, pair, :], in_=sin_v[:, pair, :])
+            if n == 0:
+                nc.sync.dma_start(out=wr[:, NJ : 2 * NJ, :], in_=w_v[:, NJ : 2 * NJ, :])
+            if n == 1:
+                nc.sync.dma_start(out=gb_raw[:], in_=sqk.partition_broadcast(P))
 
         grouped = {}
         word_banks = {}
         banks = {}
         prod_tiles = {}
-        r_banks = {}
+        r_src = {}
         norm_tiles = {}
 
         def rows_tp(key, rows):
             pts = []
             for m in range(len(rows) // 2):
-                pt = psum_tp.tile([P, 2, 2, P], F32, tag="tp", name="pt")
+                pt = psum_pt.tile([P, 2, 2, P], F32, tag="tp", name="pt")
                 pts.append(pt)
                 for i in range(2):
                     words = rows[2 * m + i].bitcast(F32)
@@ -134,7 +165,7 @@ def tile_attentionhead_pa_t_kernel(tc, input_vecs, qk_w, sqk, cos, sin, out_0, o
 
         def tab(q, is_sin):
             raw = sr if is_sin else cr
-            ptb = psum_tp.tile([P, NJ, GT], BF16, tag="tp", name="ptb")
+            ptb = psum_pt.tile([P, NJ, GT], BF16, tag="tp", name="ptb")
             for j in range(NJ):
                 for i in range(2):
                     nc.tensor.transpose(
@@ -146,42 +177,63 @@ def tile_attentionhead_pa_t_kernel(tc, input_vecs, qk_w, sqk, cos, sin, out_0, o
             else:
                 nc.scalar.copy(out=tabs[:, 0, :, q, :], in_=ptb[:])
 
+        def is_tm(g):
+            return ORDER[g][0] % NPAIR in TMQ
+
+        def mx_pass(out, cols, toks, w_first):
+            w_args = (wc[:, cols].bitcast(FP8X4), ws[:, cols])
+            x_args = (xc[:, toks].bitcast(FP8X4), xs[:, toks])
+            lhs, rhs = (w_args, x_args) if w_first else (x_args, w_args)
+            nc.tensor.matmul_mx(
+                out=out, lhsT=lhs[0], lhsT_scale=lhs[1], rhs=rhs[0], rhs_scale=rhs[1], start=True, stop=True
+            )
+
         def mx(g, dup):
-            s, h = divmod(g, 2)
-            tok = slice(s * GT, (s + 1) * GT)
+            s, h = ORDER[g]
             banks[g] = []
             for pr in range(2):
                 x2 = psum_mx.tile([P, 2, GT], F32, tag="mx", name="x2")
                 banks[g].append(x2)
-                for t2 in range(2):
-                    c0 = h * DI + (pr + 2 * t2) * P
-                    for rep in range(2 if 2 * pr + t2 < dup else 1):
-                        nc.tensor.matmul_mx(
-                            out=x2[:, t2, :],
-                            lhsT=wc[:, c0 : c0 + P].bitcast(FP8X4),
-                            lhsT_scale=ws[:, c0 : c0 + P],
-                            rhs=xc[:, tok].bitcast(FP8X4),
-                            rhs_scale=xs[:, tok],
-                            start=True,
-                            stop=True,
-                        )
+                if is_tm(g):
+                    tok = slice(s * GT + pr * P, s * GT + (pr + 1) * P)
+                    mx_pass(x2[:].rearrange("p a t -> p (a t)"), slice(h * DI, (h + 1) * DI), tok, False)
+                else:
+                    tok = slice(s * GT, (s + 1) * GT)
+                    for t2 in range(2):
+                        c0 = h * DI + (pr + 2 * t2) * P
+                        for rep in range(2 if 2 * pr + t2 < dup else 1):
+                            mx_pass(x2[:, t2, :], slice(c0, c0 + P), tok, True)
 
-        def prod(g, pr):
-            q = (g // 2) % NPAIR
-            ab = prods.tile([P, 2, 2, GT], F32, tag="ab", name="ab")
-            prod_tiles[(g, pr)] = ab
-            nc.vector.tensor_tensor(
-                out=ab[:],
-                in0=banks[g][pr][:].unsqueeze(1).to_broadcast([P, 2, 2, GT]),
-                in1=tabs[:, :, slice(pr, NJ, 2), q, :],
-                op=ALU.mult,
-            )
+        def prod(g, pr, ts):
+            s, h = ORDER[g]
+            q = s % NPAIR
+            if ts.start == 0:
+                prod_tiles[(g, pr)] = prods.tile([P, 2, 2, GT], F32, tag="ab", name="ab")
+            ab = prod_tiles[(g, pr)]
+            if is_tm(g):
+                n = 2 * q + pr
+                nc.vector.tensor_tensor(
+                    out=ab[:, 0], in0=banks[g][pr][:], in1=cr[:, n, :].rearrange("p (a t) -> p a t", a=2), op=ALU.mult
+                )
+                nc.vector.tensor_tensor(
+                    out=ab[:, 1, 0, :], in0=banks[g][pr][:, 1, :], in1=sneg[:, pr, :], op=ALU.mult
+                )
+                nc.vector.tensor_tensor(
+                    out=ab[:, 1, 1, :], in0=banks[g][pr][:, 0, :], in1=sr[:, n, H:DI], op=ALU.mult
+                )
+            else:
+                nc.vector.tensor_tensor(
+                    out=ab[:, :, :, ts],
+                    in0=banks[g][pr][:, :, ts].unsqueeze(1).to_broadcast([P, 2, 2, ts.stop - ts.start]),
+                    in1=tabs[:, :, slice(pr, NJ, 2), q, ts],
+                    op=ALU.mult,
+                )
 
         def add_t(g):
-            r_banks[g] = []
+            r_src[g] = []
             for i in range(2):
                 rb = psum_tp.tile([P, DI], F32, tag="tp", name="rb")
-                r_banks[g].append(rb)
+                r_src[g].append(rb[:])
                 ts = slice(i * P, (i + 1) * P)
                 for pr in range(2):
                     ab = prod_tiles[(g, pr)]
@@ -205,126 +257,177 @@ def tile_attentionhead_pa_t_kernel(tc, input_vecs, qk_w, sqk, cos, sin, out_0, o
                             stop=True,
                         )
 
-        def sum_squares(g, i):
-            if i == 0:
+        def out_tile(g):
+            if g not in norm_tiles:
                 ssq = small.tile([P, 2], F32, tag="ssq", name="ssq")
                 rho = small.tile([P, 2], F32, tag="rho", name="rho")
                 ot = outs.tile([P, 2, DI], F32, tag="ot", name="ot")
                 norm_tiles[g] = (ssq, rho, ot)
-            junk = stage.tile([P, DI], BF16, tag="junk", name="junk")
-            nc.scalar.activation(
-                out=junk[:], in_=r_banks[g][i][:], func=ACT.Square, accum_out=norm_tiles[g][0][:, i : i + 1]
-            )
+            return norm_tiles[g]
 
-        def inv_norm(g, i):
+        def add_g(g):
+            ssq, rho, ot = out_tile(g)
+            r_src[g] = []
+            for i in range(2):
+                ab = prod_tiles[(g, i)]
+                nc.gpsimd.tensor_tensor(
+                    out=ot[:, i, :],
+                    in0=ab[:, 0].rearrange("p a t -> p (a t)"),
+                    in1=ab[:, 1].rearrange("p a t -> p (a t)"),
+                    op=ALU.add,
+                )
+                r_src[g].append(ot[:, i, :])
+
+        def sum_squares(g, i):
+            ssq, rho, ot = out_tile(g)
+            junk = stage.tile([P, DI], BF16, tag="junk", name="junk")
+            nc.scalar.activation(out=junk[:], in_=r_src[g][i], func=ACT.Square, accum_out=ssq[:, i : i + 1])
+
+        def inv_norm(g, lo, hi):
             ssq, rho, ot = norm_tiles[g]
-            col = slice(i, i + 1)
-            nc.scalar.activation(out=rho[:, col], in_=ssq[:, col], func=ACT.Abs_reciprocal_sqrt, scale=1.0 / D)
+            if INV == "g":
+                nc.gpsimd.tensor_tensor(out=rho[:, lo:hi], in0=ssq[:, lo:hi], in1=mhalf[:, lo:hi], op=ALU.pow)
+            else:
+                nc.scalar.activation(out=rho[:, lo:hi], in_=ssq[:, lo:hi], func=ACT.Abs_reciprocal_sqrt, scale=1.0 / D)
 
         def scale_out(g, i):
             ssq, rho, ot = norm_tiles[g]
-            nc.scalar.activation(out=ot[:, i, :], in_=r_banks[g][i][:], func=ACT.Copy, scale=rho[:, i : i + 1])
-
-        def on_v(g):
-            return g % 2 == 1
-
-        def gain_store(g):
-            s, h = divmod(g, 2)
-            b, q = divmod(s, NPAIR)
-            ot = norm_tiles[g][2]
-            n = 1 if on_v(g) else 2
-            nc.gpsimd.tensor_tensor(
-                out=ot[:, 0:n, :],
-                in0=ot[:, 0:n, :],
-                in1=gb[:].unsqueeze(1).to_broadcast([P, n, DI]),
-                op=ALU.mult,
-            )
-            nc.sync.dma_start(out=o_v[h][b][:, 2 * q : 2 * q + 2, :], in_=ot[:])
-
-        def gain_store_unit(g, i):
-            s, h = divmod(g, 2)
-            b, q = divmod(s, NPAIR)
-            ot = norm_tiles[g][2]
-            nc.gpsimd.tensor_tensor(out=ot[:, i, :], in0=ot[:, i, :], in1=gb[:], op=ALU.mult)
-            nc.sync.dma_start(out=o_v[h][b][:, 2 * q + i, :], in_=ot[:, i, :])
+            nc.scalar.activation(out=ot[:, i, :], in_=r_src[g][i], func=ACT.Copy, scale=rho[:, i : i + 1])
 
         def norm_gain_on_v(g, i):
             ssq, rho, ot = norm_tiles[g]
             nc.vector.scalar_tensor_tensor(
-                out=ot[:, i, :],
-                in0=r_banks[g][i][:],
-                scalar=rho[:, i : i + 1],
-                in1=gb[:],
-                op0=ALU.mult,
-                op1=ALU.mult,
+                out=ot[:, i, :], in0=r_src[g][i], scalar=rho[:, i : i + 1], in1=gb[:], op0=ALU.mult, op1=ALU.mult
             )
 
-        def last_unit(g, i):
-            s, h = divmod(g, 2)
-            b, q = divmod(s, NPAIR)
+        def gain(g, lo, hi):
             ot = norm_tiles[g][2]
-            norm_gain_on_v(g, i)
-            nc.sync.dma_start(out=o_v[h][b][:, 2 * q + i, :], in_=ot[:, i, :])
+            nc.gpsimd.tensor_tensor(
+                out=ot[:, lo:hi, :],
+                in0=ot[:, lo:hi, :],
+                in1=gb[:].unsqueeze(1).to_broadcast([P, hi - lo, DI]),
+                op=ALU.mult,
+            )
 
-        def finish(g):
-            last = g == NG - 1
-            sum_squares(g, 0)
-            if last:
-                last_unit(g - 1, 1)
-            elif g >= 1:
-                if not on_v(g - 1):
-                    scale_out(g - 1, 1)
-                gain_store(g - 1)
-            inv_norm(g, 0)
-            if last:
-                last_unit(g, 0)
-            sum_squares(g, 1)
-            if not last:
-                scale_out(g, 0)
-            if g == NG - 2:
-                gain_store_unit(g, 0)
-            inv_norm(g, 1)
-            if last:
-                last_unit(g, 1)
+        def store(g, lo, hi):
+            s, h = ORDER[g]
+            b, q = divmod(s, NPAIR)
+            nc.sync.dma_start(out=o_v[h][b][:, 2 * q + lo : 2 * q + hi, :], in_=norm_tiles[g][2][:, lo:hi, :])
+
+        cm_groups = [g for g in range(NG) if not is_tm(g)]
+        on_v = set(g for n, g in enumerate(cm_groups) if (n * ONV) // 10 != ((n + 1) * ONV) // 10)
+        first_use = {s: min(g for g in range(NG) if ORDER[g][0] == s) for s in x_order}
 
         w_tp(0)
-        spin(1)
         rows_ev(("w", 0), (False, True))
+        spin(1)
         x_tp(0)
         rows_ev(("x", 0), (False,))
         w_q(0)
         x_q(0)
-        w_tp(1)
-        spin(1)
-        rows_ev(("w", 1), (True, False))
-        w_q(1)
         tab(0, False)
         spin(1)
         tab(0, True)
         spin(1)
         mx(0, 0)
-        x_tp(1)
-        rows_ev(("x", 1), (True,))
+        w_tp(1)
+        spin(1)
 
-        tab_at = {0: ((1, False), (1, True)), 1: ((2, False),), 2: ((2, True),), 3: ((3, False),), 4: ((3, True),)}
+        tab_at = {}
+        for q in range(1, NPAIR):
+            if q not in TMQ:
+                first = min(g for g in range(NG) if ORDER[g][0] % NPAIR == q)
+                for is_sin in range(2):
+                    tab_at.setdefault(max(0, first - TLEAD - 1 + is_sin), []).append((q, bool(is_sin)))
+        sq_at = {}
+        for g in range(NG):
+            sq_at.setdefault(g + (2 if is_tm(g) else 1), []).append(g)
+        before = None
+
+        def finish(g, i):
+            if is_tm(g) and G_SCALE:
+                ssq, rho, ot = norm_tiles[g]
+                nc.gpsimd.tensor_scalar(
+                    out=ot[:, i, :], in0=ot[:, i, :], scalar1=rho[:, i : i + 1], scalar2=0.0, op0=ALU.mult, op1=ALU.add
+                )
+                if i == 1:
+                    gain(g, 0, 2)
+                    store(g, 0, 2)
+            elif g >= NG - 1 or (g == NG - 2 and i == 1):
+                norm_gain_on_v(g, i)
+                store(g, i, i + 1)
+            elif i == 0 or g not in on_v:
+                scale_out(g, i)
+                if i == 1 or g in on_v:
+                    gain(g, 0, i + 1)
+                    store(g, 0, i + 1)
+                if g == NG - 2:
+                    gain(g, i, i + 1)
+                    store(g, i, i + 1)
+
         for it in range(NG + 1):
-            s_new = (it + 3) // 2 if it % 2 == 1 and (it + 3) // 2 < NS else None
-            if it >= 1:
-                add_t(it - 1)
-            if s_new is not None:
-                x_tp(s_new)
-            if it < NG:
-                prod(it, 0)
-                if it >= 2 and on_v(it - 2):
-                    norm_gain_on_v(it - 2, 1)
-                prod(it, 1)
-            if it % 2 == 0 and (it + 2) // 2 < NS:
-                x_q((it + 2) // 2)
-            if it + 1 < NG:
+            last = NG - 1
+            if MX_FIRST and it + 1 < NG and it > 0:
                 mx(it + 1, DUP)
-            if it >= 1:
-                finish(it - 1)
-            if s_new is not None:
-                rows_ev(("x", s_new), (True,))
+            if 1 <= it <= NG and not is_tm(it - 1):
+                add_t(it - 1)
+            s_tp = [s for s in x_order if s > 0 and max(0, first_use[s] - LEADT) == it]
+            for s in s_tp:
+                x_tp(s)
+            s_q = [s for s in x_order if s > 0 and max(0, first_use[s] - LEADQ) == it]
+            if it == last:
+                for half in range(2):
+                    for pr in range(2):
+                        prod(it, pr, slice(half * P, (half + 1) * P))
+            elif it < last:
+                prod(it, 0, slice(0, GT))
+                if it == 0:
+                    rows_ev(("w", 1), (True, False))
+                    w_q(1)
+                prod(it, 1, slice(0, GT))
+            if it == 0:
+                x_ev = s_tp
+                for s in s_tp:
+                    rows_ev(("x", s), (XEV,))
+            for s in s_q:
+                x_q(s)
+            if it - 2 in on_v:
+                norm_gain_on_v(it - 2, 1)
+                store(it - 2, 1, 2)
+            if it + 1 < NG and (it == 0 or not MX_FIRST):
+                mx(it + 1, DUP)
+            if it < NG and is_tm(it):
+                add_g(it)
+            for g in sq_at.get(it, []):
+                if INV == "s":
+                    for i in range(2):
+                        sum_squares(g, i)
+                        if before is not None:
+                            finish(*before)
+                        inv_norm(g, i, i + 1)
+                        before = (g, i)
+                else:
+                    for i in range(2):
+                        sum_squares(g, i)
+                        if g == last:
+                            inv_norm(g, i, i + 1)
+                        if before is not None:
+                            finish(before, i)
+                        if g == last:
+                            finish(g, i)
+                    if g < last:
+                        inv_norm(g, 0, 2)
+                    before = g
+            if it == NG and INV == "s":
+                finish(*before)
+            if it > 0:
+                for s in s_tp:
+                    rows_ev(("x", s), (XEV,))
+            if it == 0 and INV == "g":
+                nc.scalar.mul(out=gb[:], in_=gb_raw[:], mul=math.sqrt(D))
+            if it == 0 and TMQ:
+                nc.gpsimd.tensor_scalar(
+                    out=sneg[:], in0=sr[:, 6:8, 0:H], scalar1=-1.0, scalar2=0.0, op0=ALU.mult, op1=ALU.add
+                )
             for q, is_sin in tab_at.get(it, ()):
                 tab(q, is_sin)

@@ -1,4 +1,3 @@
-import math
 from contextlib import ExitStack
 
 import concourse.mybir as mybir
@@ -14,40 +13,36 @@ ALU = mybir.AluOpType
 
 P = 128
 B, T, D, DI = 4, 1024, 512, 512
-H = DI // 2
 NT = T // P
 NPAIR = NT // 2
 NJ = DI // P
 GT = 2 * P
 NS = B * NPAIR
-TMQ = ()
-NC = NPAIR - len(TMQ)
+NG = 2 * NS
 DUP = 0
-PLAIN = (2, 5)
-ONV = 8
-INV = "s"
-TLEAD = 2
-XEV = True
-G_SCALE = False
-MX_FIRST = False
+PLAIN = ()
+VFIRST = 1
+VSTEP = 2
 BMX = 3
 BR = 5
-BPT = 0
-LEADT = 3
-LEADQ = 2
-SPIN_FIRST = 3
+TLEAD = 6
+TSTEP = 2
+XFIRST = True
+XEVI = 0
+HQ = True
+HM = False
+NEG_G = True
+WEV = (False, True, True, True)
+XSV = 0
+SPIN_FIRST = 4
+HSPIN = 1
 FLOPS = 2 * B * T * D * 2 * DI
-
-BORDER = ((0, 0), (0, 1), (1, 0), (3, 0), (1, 1), (2, 0), (3, 1), (2, 1))
-QMAJOR = True
-ORDER = [(b * NPAIR + q, h) for q in range(NPAIR) for b in range(B) for h in range(2)] if QMAJOR else [(batch * NPAIR + pair, half) for batch in range(B) for pair, half in (BORDER if TMQ else [(a, c) for a in range(4) for c in range(2)])]
-NG = len(ORDER)
 
 
 def tile_attentionhead_pa_t_kernel(tc, input_vecs, qk_w, sqk, cos, sin, out_0, out_1):
     nc = tc.nc
     x_v = input_vecs.rearrange("b (p n) k -> b p n k", n=NT)
-    w_v = qk_w.rearrange("(r p) k -> p r k", p=P)
+    w_v = qk_w.rearrange("(h t r p) k -> p h r t k", p=P, r=2, t=2)
     cos_v = cos.rearrange("(p n) c -> p n c", n=NT)
     sin_v = sin.rearrange("(p n) c -> p n c", n=NT)
     o_v = [o.rearrange("b (p n) c -> b p n c", n=NT) for o in (out_0, out_1)]
@@ -56,27 +51,60 @@ def tile_attentionhead_pa_t_kernel(tc, input_vecs, qk_w, sqk, cos, sin, out_0, o
         const = ctx.enter_context(tc.tile_pool(name="const", bufs=1))
         stage = ctx.enter_context(tc.tile_pool(name="stage", bufs=3))
         prods = ctx.enter_context(tc.tile_pool(name="prods", bufs=6))
-        outs = ctx.enter_context(tc.tile_pool(name="outs", bufs=7))
-        small = ctx.enter_context(tc.tile_pool(name="small", bufs=8))
+        outs = ctx.enter_context(tc.tile_pool(name="outs", bufs=6))
+        small = ctx.enter_context(tc.tile_pool(name="small", bufs=6))
         psum_mx = ctx.enter_context(tc.psum_pool(name="psum_mx", bufs=BMX))
         psum_tp = ctx.enter_context(tc.psum_pool(name="psum_tp", bufs=BR))
-        psum_pt = ctx.enter_context(tc.psum_pool(name="psum_pt", bufs=BPT)) if BPT else psum_tp
         ctx.enter_context(tc.manual_schedule())
 
-        ident_f = const.tile([P, P], F32, name="ident_f")
-        make_identity(nc, ident_f[:])
-        ident_b = const.tile([P, P], BF16, name="ident_b")
-        make_identity(nc, ident_b[:])
-        mhalf = const.tile([P, 2], F32, name="mhalf")
-        nc.vector.memset(mhalf[:], -0.5)
-        one = const.tile([P, 1], F32, name="one")
-        nc.vector.memset(one[:], 1.0)
-        warm = const.tile([P, 1], F32, name="warm")
-        nc.scalar.activation(out=warm[:], in_=one[:], func=ACT.Square if INV == "g" else ACT.Abs_reciprocal_sqrt)
+        xr = const.tile([P, NS, 2, D], BF16, name="xr")
+        wr = const.tile([P, 2, 2, 2, D], BF16, name="wr")
+        cr = const.tile([P, NT, DI], BF16, name="cr")
+        sr = const.tile([P, NT, DI], BF16, name="sr")
+        gb = const.tile([P, DI], BF16, name="gb")
+        xc = const.tile([P, B * T], U32, name="xc", align_bytes=64)
+        xs = const.tile([P, B * T], U8, name="xs", align_bytes=64)
+        wc = const.tile([P, 2 * DI], U32, name="wc", align_bytes=64)
+        ws = const.tile([P, 2 * DI], U8, name="ws", align_bytes=64)
+        tabs = const.tile([P, NPAIR, 2, 2, 2, GT], BF16, name="tabs")
+
+        def load_w(h, pr):
+            nc.sync.dma_start(out=wr[:, h, pr], in_=w_v[:, h, pr])
+
+        def load_x(n):
+            q, b = divmod(n, B)
+            nc.sync.dma_start(out=xr[:, n], in_=x_v[b][:, 2 * q : 2 * q + 2, :])
+
+        def load_tab(q):
+            pair = slice(2 * q, 2 * q + 2)
+            nc.sync.dma_start(out=cr[:, pair, :], in_=cos_v[:, pair, :])
+            nc.sync.dma_start(out=sr[:, pair, :], in_=sin_v[:, pair, :])
+
+        load_w(0, 0)
+        load_x(0)
+        load_tab(0)
+        load_w(0, 1)
+        load_w(1, 0)
+        load_w(1, 1)
+        load_x(1)
+        nc.sync.dma_start(out=gb[:], in_=sqk.partition_broadcast(P))
+        for n in range(2, NS):
+            load_x(n)
+            if n % B == 2 and n // B + 1 < NPAIR:
+                load_tab(n // B + 1)
+
         zl = const.tile([P, P], BF16, name="zl")
         nc.vector.memset(zl[:], 0.0)
         zr = const.tile([P, 2 * GT], BF16, name="zr")
         nc.vector.memset(zr[:], 0.0)
+        ident_f = const.tile([P, P], F32, name="ident_f")
+        make_identity(nc, ident_f[:])
+        ident_b = const.tile([P, P], BF16, name="ident_b")
+        make_identity(nc, ident_b[:])
+        one = const.tile([P, 1], F32, name="one")
+        nc.vector.memset(one[:], 1.0)
+        warm = const.tile([P, 1], F32, name="warm")
+        nc.scalar.activation(out=warm[:], in_=one[:], func=ACT.Abs_reciprocal_sqrt)
         dm = psum_mx.tile([P, 2 * GT], F32, tag="mx", name="dm")
 
         def spin(n):
@@ -85,219 +113,152 @@ def tile_attentionhead_pa_t_kernel(tc, input_vecs, qk_w, sqk, cos, sin, out_0, o
 
         spin(SPIN_FIRST)
 
-        xr = [const.tile([P, NT, D], BF16, name="xr%d" % b) for b in range(B)]
-        wr = const.tile([P, 2 * NJ, D], BF16, name="wr")
-        cr = const.tile([P, NT, DI], BF16, name="cr")
-        sr = const.tile([P, NT, DI], BF16, name="sr")
-        gb_raw = const.tile([P, DI], BF16, name="gb_raw")
-        gb = const.tile([P, DI], F32, name="gb") if INV == "g" else gb_raw
-        sneg = const.tile([P, 2, H], BF16, name="sneg")
-        xc = const.tile([P, B * T], U32, name="xc", align_bytes=64)
-        xs = const.tile([P, B * T], U8, name="xs", align_bytes=64)
-        wc = const.tile([P, 2 * DI], U32, name="wc", align_bytes=64)
-        ws = const.tile([P, 2 * DI], U8, name="ws", align_bytes=64)
-        tabs = const.tile([P, 2, NJ, NC, GT], BF16, name="tabs")
-
-        nc.sync.dma_start(out=wr[:, 0:2, :], in_=w_v[:, 0:2, :])
-        nc.sync.dma_start(out=wr[:, 2:NJ, :], in_=w_v[:, 2:NJ, :])
-        x_order = []
-        for s, h in ORDER:
-            if s not in x_order:
-                x_order.append(s)
-        q_seen = []
-        for n, s in enumerate(x_order):
-            b, q = divmod(s, NPAIR)
-            pair = slice(2 * q, 2 * q + 2)
-            nc.sync.dma_start(out=xr[b][:, pair, :], in_=x_v[b][:, pair, :])
-            if q not in q_seen:
-                q_seen.append(q)
-                nc.sync.dma_start(out=cr[:, pair, :], in_=cos_v[:, pair, :])
-                nc.sync.dma_start(out=sr[:, pair, :], in_=sin_v[:, pair, :])
-            if n == 0:
-                nc.sync.dma_start(out=wr[:, NJ : 2 * NJ, :], in_=w_v[:, NJ : 2 * NJ, :])
-            if n == 1:
-                nc.sync.dma_start(out=gb_raw[:], in_=sqk.partition_broadcast(P))
-
         grouped = {}
         word_banks = {}
         banks = {}
         prod_tiles = {}
-        r_src = {}
+        r_banks = {}
         norm_tiles = {}
 
         def rows_tp(key, rows):
-            pts = []
-            for m in range(len(rows) // 2):
-                pt = psum_pt.tile([P, 2, 2, P], F32, tag="tp", name="pt")
-                pts.append(pt)
-                for i in range(2):
-                    words = rows[2 * m + i].bitcast(F32)
-                    for u in range(2):
-                        nc.tensor.transpose(pt[:, i, u, :], words[:, u : 2 * P : 2], ident_f[:])
-            word_banks[key] = pts
+            pt = psum_tp.tile([P, 2, 2, P], F32, tag="tp", name="pt")
+            word_banks[key] = pt
+            for i in range(2):
+                words = rows[i].bitcast(F32)
+                for u in range(2):
+                    nc.tensor.transpose(pt[:, i, u, :], words[:, u : D // 2 : 2], ident_f[:])
 
         def rows_ev(key, on_scalar):
-            pts = word_banks[key]
-            g_t = stage.tile([P, len(pts) * 2 * P * 4], BF16, tag="g%d" % len(pts), name="g_t", align_bytes=64)
+            g_t = stage.tile([P, 2 * P * 4], BF16, tag="g", name="g_t", align_bytes=64)
             grouped[key] = g_t
-            gw = g_t[:].bitcast(F32).rearrange("p (m i r u) -> p m i r u", i=2, r=P, u=2)
-            for m in range(len(pts)):
-                src = pts[m][:].rearrange("p i u r -> p i r u")
-                if on_scalar[m]:
-                    nc.scalar.copy(out=gw[:, m], in_=src)
-                else:
-                    nc.vector.tensor_copy(out=gw[:, m], in_=src)
+            gw = g_t[:].bitcast(F32).rearrange("p (i r u) -> p i r u", i=2, u=2)
+            src = word_banks[key][:].rearrange("p i u r -> p i r u")
+            if on_scalar:
+                nc.scalar.copy(out=gw, in_=src)
+            else:
+                nc.vector.tensor_copy(out=gw, in_=src)
 
-        def w_tp(h):
-            rows_tp(("w", h), [wr[:, h * NJ + j, :] for j in range(NJ)])
+        def w_tp(h, pr):
+            rows_tp(("w", h, pr), [wr[:, h, pr, t, :] for t in range(2)])
 
-        def w_q(h):
-            cols = slice(h * DI, (h + 1) * DI)
-            nc.vector.quantize_mx(out=wc[:, cols].bitcast(FP8X4), scales=ws[:, cols], in_=grouped[("w", h)][:])
+        def w_ev(h, pr):
+            rows_ev(("w", h, pr), WEV[2 * h + pr])
 
-        def x_tp(s):
-            b, q = divmod(s, NPAIR)
-            rows_tp(("x", s), [xr[b][:, 2 * q + i, :] for i in range(2)])
+        def w_q(h, pr):
+            cols = slice((2 * h + pr) * GT, (2 * h + pr + 1) * GT)
+            nc.vector.quantize_mx(out=wc[:, cols].bitcast(FP8X4), scales=ws[:, cols], in_=grouped[("w", h, pr)][:])
 
-        def x_q(s):
-            cols = slice(s * GT, (s + 1) * GT)
-            nc.vector.quantize_mx(out=xc[:, cols].bitcast(FP8X4), scales=xs[:, cols], in_=grouped[("x", s)][:])
+        def x_tp(n):
+            rows_tp(n, [xr[:, n, i, :] for i in range(2)])
 
-        def tab(q, is_sin):
-            raw = sr if is_sin else cr
-            ptb = psum_pt.tile([P, NJ, GT], BF16, tag="tp", name="ptb")
-            for j in range(NJ):
+        def x_q(n):
+            cols = slice(n * GT, (n + 1) * GT)
+            nc.vector.quantize_mx(out=xc[:, cols].bitcast(FP8X4), scales=xs[:, cols], in_=grouped[n][:])
+
+        def tab(q, pr):
+            ptb = psum_tp.tile([P, 4, GT], BF16, tag="tp", name="ptb")
+            for n, (raw, j) in enumerate(((cr, pr), (cr, pr + 2), (sr, pr + 2), (sr, pr))):
                 for i in range(2):
                     nc.tensor.transpose(
-                        ptb[:, j, i * P : (i + 1) * P], raw[:, 2 * q + i, j * P : (j + 1) * P], ident_b[:]
+                        ptb[:, n, i * P : (i + 1) * P], raw[:, 2 * q + i, j * P : (j + 1) * P], ident_b[:]
                     )
-            if is_sin:
-                nc.scalar.copy(out=tabs[:, 1, 0:2, q, :], in_=ptb[:, 2:4, :])
-                nc.scalar.mul(out=tabs[:, 1, 2:4, q, :], in_=ptb[:, 0:2, :], mul=-1.0)
+            out = tabs[:, q, pr].rearrange("p c t r -> p (c t) r")
+            if q == 0 or not NEG_G:
+                nc.scalar.copy(out=out[:, 0:3], in_=ptb[:, 0:3])
+                nc.scalar.mul(out=out[:, 3], in_=ptb[:, 3], mul=-1.0)
             else:
-                nc.scalar.copy(out=tabs[:, 0, :, q, :], in_=ptb[:])
+                nc.scalar.copy(out=out, in_=ptb[:])
 
-        def is_tm(g):
-            return ORDER[g][0] % NPAIR in TMQ
+        def negate(q):
+            half = sr[:, 2 * q : 2 * q + 2, 0 : DI // 2]
+            nc.gpsimd.tensor_scalar(out=half, in0=half, scalar1=-1.0, scalar2=0.0, op0=ALU.mult, op1=ALU.add)
 
-        def mx_pass(out, cols, toks, w_first):
-            w_args = (wc[:, cols].bitcast(FP8X4), ws[:, cols])
-            x_args = (xc[:, toks].bitcast(FP8X4), xs[:, toks])
-            lhs, rhs = (w_args, x_args) if w_first else (x_args, w_args)
-            nc.tensor.matmul_mx(
-                out=out, lhsT=lhs[0], lhsT_scale=lhs[1], rhs=rhs[0], rhs_scale=rhs[1], start=True, stop=True
-            )
+        def mx(g, pr):
+            n, h = divmod(g, 2)
+            tok = slice(n * GT, (n + 1) * GT)
+            x2 = psum_mx.tile([P, 2, GT], F32, tag="mx", name="x2")
+            banks[(g, pr)] = x2
+            for t in range(2):
+                c0 = ((2 * h + pr) * 2 + t) * P
+                for rep in range(2 if 2 * pr + t < DUP and g > 0 else 1):
+                    nc.tensor.matmul_mx(
+                        out=x2[:, t, :],
+                        lhsT=wc[:, c0 : c0 + P].bitcast(FP8X4),
+                        lhsT_scale=ws[:, c0 : c0 + P],
+                        rhs=xc[:, tok].bitcast(FP8X4),
+                        rhs_scale=xs[:, tok],
+                        start=True,
+                        stop=True,
+                    )
 
-        def mx(g, dup):
-            s, h = ORDER[g]
-            banks[g] = []
-            for pr in range(2):
-                x2 = psum_mx.tile([P, 2, GT], F32, tag="mx", name="x2")
-                banks[g].append(x2)
-                if is_tm(g):
-                    tok = slice(s * GT + pr * P, s * GT + (pr + 1) * P)
-                    mx_pass(x2[:].rearrange("p a t -> p (a t)"), slice(h * DI, (h + 1) * DI), tok, False)
-                else:
-                    tok = slice(s * GT, (s + 1) * GT)
-                    for t2 in range(2):
-                        c0 = h * DI + (pr + 2 * t2) * P
-                        for rep in range(2 if 2 * pr + t2 < dup else 1):
-                            mx_pass(x2[:, t2, :], slice(c0, c0 + P), tok, True)
-
-        def prod(g, pr, ts):
-            s, h = ORDER[g]
-            q = s % NPAIR
+        def prod(g, pr, ts=slice(0, GT)):
+            q = g // (2 * B)
             if ts.start == 0:
                 prod_tiles[(g, pr)] = prods.tile([P, 2, 2, GT], F32, tag="ab", name="ab")
-            ab = prod_tiles[(g, pr)]
-            if is_tm(g):
-                n = 2 * q + pr
-                nc.vector.tensor_tensor(
-                    out=ab[:, 0], in0=banks[g][pr][:], in1=cr[:, n, :].rearrange("p (a t) -> p a t", a=2), op=ALU.mult
-                )
-                nc.vector.tensor_tensor(
-                    out=ab[:, 1, 0, :], in0=banks[g][pr][:, 1, :], in1=sneg[:, pr, :], op=ALU.mult
-                )
-                nc.vector.tensor_tensor(
-                    out=ab[:, 1, 1, :], in0=banks[g][pr][:, 0, :], in1=sr[:, n, H:DI], op=ALU.mult
-                )
-            else:
-                nc.vector.tensor_tensor(
-                    out=ab[:, :, :, ts],
-                    in0=banks[g][pr][:, :, ts].unsqueeze(1).to_broadcast([P, 2, 2, ts.stop - ts.start]),
-                    in1=tabs[:, :, slice(pr, NJ, 2), q, ts],
-                    op=ALU.mult,
-                )
+            nc.vector.tensor_tensor(
+                out=prod_tiles[(g, pr)][:, :, :, ts],
+                in0=banks[(g, pr)][:, :, ts].unsqueeze(1).to_broadcast([P, 2, 2, ts.stop - ts.start]),
+                in1=tabs[:, q, pr, :, :, ts],
+                op=ALU.mult,
+            )
 
         def add_t(g):
-            r_src[g] = []
+            r_banks[g] = []
             for i in range(2):
                 rb = psum_tp.tile([P, DI], F32, tag="tp", name="rb")
-                r_src[g].append(rb[:])
+                r_banks[g].append(rb)
                 ts = slice(i * P, (i + 1) * P)
                 for pr in range(2):
                     ab = prod_tiles[(g, pr)]
-                    for t2 in range(2):
-                        j = pr + 2 * t2
+                    for t in range(2):
+                        j = pr + 2 * t
                         cs = slice(j * P, (j + 1) * P)
                         nc.tensor.matmul(
                             out=rb[:, cs],
-                            lhsT=ab[:, 0, t2, ts],
+                            lhsT=ab[:, 0, t, ts],
                             rhs=ident_f[:],
-                            is_transpose=4 * i + 2 * pr + t2 not in PLAIN,
+                            is_transpose=4 * i + 2 * pr + t not in PLAIN,
                             start=True,
                             stop=False,
                         )
                         nc.tensor.matmul(
                             out=rb[:, cs],
-                            lhsT=ab[:, 1, 1 - t2, ts],
+                            lhsT=ab[:, 1, 1 - t, ts],
                             rhs=ident_f[:],
                             is_transpose=True,
                             start=False,
                             stop=True,
                         )
 
-        def out_tile(g):
-            if g not in norm_tiles:
+        def sum_squares(g, i):
+            if i == 0:
                 ssq = small.tile([P, 2], F32, tag="ssq", name="ssq")
                 rho = small.tile([P, 2], F32, tag="rho", name="rho")
                 ot = outs.tile([P, 2, DI], F32, tag="ot", name="ot")
                 norm_tiles[g] = (ssq, rho, ot)
-            return norm_tiles[g]
-
-        def add_g(g):
-            ssq, rho, ot = out_tile(g)
-            r_src[g] = []
-            for i in range(2):
-                ab = prod_tiles[(g, i)]
-                nc.gpsimd.tensor_tensor(
-                    out=ot[:, i, :],
-                    in0=ab[:, 0].rearrange("p a t -> p (a t)"),
-                    in1=ab[:, 1].rearrange("p a t -> p (a t)"),
-                    op=ALU.add,
-                )
-                r_src[g].append(ot[:, i, :])
-
-        def sum_squares(g, i):
-            ssq, rho, ot = out_tile(g)
             junk = stage.tile([P, DI], BF16, tag="junk", name="junk")
-            nc.scalar.activation(out=junk[:], in_=r_src[g][i], func=ACT.Square, accum_out=ssq[:, i : i + 1])
+            nc.scalar.activation(
+                out=junk[:], in_=r_banks[g][i][:], func=ACT.Square, accum_out=norm_tiles[g][0][:, i : i + 1]
+            )
 
-        def inv_norm(g, lo, hi):
+        def inv_norm(g, i):
             ssq, rho, ot = norm_tiles[g]
-            if INV == "g":
-                nc.gpsimd.tensor_tensor(out=rho[:, lo:hi], in0=ssq[:, lo:hi], in1=mhalf[:, lo:hi], op=ALU.pow)
-            else:
-                nc.scalar.activation(out=rho[:, lo:hi], in_=ssq[:, lo:hi], func=ACT.Abs_reciprocal_sqrt, scale=1.0 / D)
+            col = slice(i, i + 1)
+            nc.scalar.activation(out=rho[:, col], in_=ssq[:, col], func=ACT.Abs_reciprocal_sqrt, scale=1.0 / D)
 
         def scale_out(g, i):
             ssq, rho, ot = norm_tiles[g]
-            nc.scalar.activation(out=ot[:, i, :], in_=r_src[g][i], func=ACT.Copy, scale=rho[:, i : i + 1])
+            nc.scalar.activation(out=ot[:, i, :], in_=r_banks[g][i][:], func=ACT.Copy, scale=rho[:, i : i + 1])
 
         def norm_gain_on_v(g, i):
             ssq, rho, ot = norm_tiles[g]
             nc.vector.scalar_tensor_tensor(
-                out=ot[:, i, :], in0=r_src[g][i], scalar=rho[:, i : i + 1], in1=gb[:], op0=ALU.mult, op1=ALU.mult
+                out=ot[:, i, :],
+                in0=r_banks[g][i][:],
+                scalar=rho[:, i : i + 1],
+                in1=gb[:],
+                op0=ALU.mult,
+                op1=ALU.mult,
             )
 
         def gain(g, lo, hi):
@@ -310,124 +271,104 @@ def tile_attentionhead_pa_t_kernel(tc, input_vecs, qk_w, sqk, cos, sin, out_0, o
             )
 
         def store(g, lo, hi):
-            s, h = ORDER[g]
-            b, q = divmod(s, NPAIR)
+            n, h = divmod(g, 2)
+            q, b = divmod(n, B)
             nc.sync.dma_start(out=o_v[h][b][:, 2 * q + lo : 2 * q + hi, :], in_=norm_tiles[g][2][:, lo:hi, :])
 
-        cm_groups = [g for g in range(NG) if not is_tm(g)]
-        on_v = set(g for n, g in enumerate(cm_groups) if (n * ONV) // 10 != ((n + 1) * ONV) // 10)
-        first_use = {s: min(g for g in range(NG) if ORDER[g][0] == s) for s in x_order}
+        def on_v(g):
+            return g >= VFIRST and (g - VFIRST) % VSTEP == 0
 
-        w_tp(0)
-        rows_ev(("w", 0), (False, True))
-        spin(1)
+        last = NG - 1
+
+        def finish(g, i):
+            if g == last or (g == last - 1 and i == 1):
+                norm_gain_on_v(g, i)
+                store(g, i, i + 1)
+            elif g == last - 1:
+                scale_out(g, i)
+                gain(g, i, i + 1)
+                store(g, i, i + 1)
+            elif i == 0 or not on_v(g):
+                scale_out(g, i)
+                if i == 1 or on_v(g):
+                    gain(g, 0, i + 1)
+                    store(g, 0, i + 1)
+
+        w_tp(0, 0)
+        w_ev(0, 0)
         x_tp(0)
-        rows_ev(("x", 0), (False,))
-        w_q(0)
+        rows_ev(0, False)
+        tab(0, 0)
+        w_q(0, 0)
         x_q(0)
-        tab(0, False)
-        spin(1)
-        tab(0, True)
-        spin(1)
-        mx(0, 0)
-        w_tp(1)
-        spin(1)
+        spin(HSPIN)
+        if HM:
+            mx(0, 0)
+        w_tp(0, 1)
+        w_ev(0, 1)
+        if not HM:
+            mx(0, 0)
+        tab(0, 1)
+        if HQ:
+            w_q(0, 1)
+        prod(0, 0)
+        if not HQ:
+            w_q(0, 1)
+        spin(HSPIN)
+        w_tp(1, 0)
+        w_ev(1, 0)
+        mx(0, 1)
+        w_tp(1, 1)
+        w_ev(1, 1)
+        w_q(1, 0)
+        prod(0, 1)
+        x_tp(1)
+        rows_ev(1, True)
+        mx(1, 0)
+        w_q(1, 1)
+        x_q(1)
+        mx(1, 1)
+        for q in range(1, NPAIR):
+            if NEG_G:
+                negate(q)
 
         tab_at = {}
         for q in range(1, NPAIR):
-            if q not in TMQ:
-                first = min(g for g in range(NG) if ORDER[g][0] % NPAIR == q)
-                for is_sin in range(2):
-                    tab_at.setdefault(max(0, first - TLEAD - 1 + is_sin), []).append((q, bool(is_sin)))
-        sq_at = {}
-        for g in range(NG):
-            sq_at.setdefault(g + (2 if is_tm(g) else 1), []).append(g)
+            for pr in range(2):
+                tab_at[2 * B * q - TLEAD + TSTEP * pr] = (q, pr)
         before = None
-
-        def finish(g, i):
-            if is_tm(g) and G_SCALE:
-                ssq, rho, ot = norm_tiles[g]
-                nc.gpsimd.tensor_scalar(
-                    out=ot[:, i, :], in0=ot[:, i, :], scalar1=rho[:, i : i + 1], scalar2=0.0, op0=ALU.mult, op1=ALU.add
-                )
-                if i == 1:
-                    gain(g, 0, 2)
-                    store(g, 0, 2)
-            elif g >= NG - 1 or (g == NG - 2 and i == 1):
-                norm_gain_on_v(g, i)
-                store(g, i, i + 1)
-            elif i == 0 or g not in on_v:
-                scale_out(g, i)
-                if i == 1 or g in on_v:
-                    gain(g, 0, i + 1)
-                    store(g, 0, i + 1)
-                if g == NG - 2:
-                    gain(g, i, i + 1)
-                    store(g, i, i + 1)
-
-        for it in range(NG + 1):
-            last = NG - 1
-            if MX_FIRST and it + 1 < NG and it > 0:
-                mx(it + 1, DUP)
-            if 1 <= it <= NG and not is_tm(it - 1):
-                add_t(it - 1)
-            s_tp = [s for s in x_order if s > 0 and max(0, first_use[s] - LEADT) == it]
-            for s in s_tp:
-                x_tp(s)
-            s_q = [s for s in x_order if s > 0 and max(0, first_use[s] - LEADQ) == it]
+        for it in range(1, NG + 1):
+            new = (it + 3) // 2 if it % 2 == 1 and (it + 3) // 2 < NS else None
+            if new is not None and XFIRST:
+                x_tp(new)
+            add_t(it - 1)
+            if new is not None and not XFIRST:
+                x_tp(new)
             if it == last:
                 for half in range(2):
                     for pr in range(2):
                         prod(it, pr, slice(half * P, (half + 1) * P))
             elif it < last:
-                prod(it, 0, slice(0, GT))
-                if it == 0:
-                    rows_ev(("w", 1), (True, False))
-                    w_q(1)
-                prod(it, 1, slice(0, GT))
-            if it == 0:
-                x_ev = s_tp
-                for s in s_tp:
-                    rows_ev(("x", s), (XEV,))
-            for s in s_q:
-                x_q(s)
-            if it - 2 in on_v:
+                prod(it, 0)
+                prod(it, 1)
+            if it % 2 == 0 and (it + 2) // 2 < NS:
+                x_q((it + 2) // 2)
+            if it >= 2 and it - 2 < last - 1 and on_v(it - 2):
                 norm_gain_on_v(it - 2, 1)
                 store(it - 2, 1, 2)
-            if it + 1 < NG and (it == 0 or not MX_FIRST):
-                mx(it + 1, DUP)
-            if it < NG and is_tm(it):
-                add_g(it)
-            for g in sq_at.get(it, []):
-                if INV == "s":
-                    for i in range(2):
-                        sum_squares(g, i)
-                        if before is not None:
-                            finish(*before)
-                        inv_norm(g, i, i + 1)
-                        before = (g, i)
-                else:
-                    for i in range(2):
-                        sum_squares(g, i)
-                        if g == last:
-                            inv_norm(g, i, i + 1)
-                        if before is not None:
-                            finish(before, i)
-                        if g == last:
-                            finish(g, i)
-                    if g < last:
-                        inv_norm(g, 0, 2)
-                    before = g
-            if it == NG and INV == "s":
-                finish(*before)
-            if it > 0:
-                for s in s_tp:
-                    rows_ev(("x", s), (XEV,))
-            if it == 0 and INV == "g":
-                nc.scalar.mul(out=gb[:], in_=gb_raw[:], mul=math.sqrt(D))
-            if it == 0 and TMQ:
-                nc.gpsimd.tensor_scalar(
-                    out=sneg[:], in0=sr[:, 6:8, 0:H], scalar1=-1.0, scalar2=0.0, op0=ALU.mult, op1=ALU.add
-                )
-            for q, is_sin in tab_at.get(it, ()):
-                tab(q, is_sin)
+            if it + 1 < NG:
+                mx(it + 1, 0)
+                mx(it + 1, 1)
+            for i in range(2):
+                sum_squares(it - 1, i)
+                if before is not None:
+                    finish(*before)
+                if new is not None and i == XEVI:
+                    rows_ev(new, XSV == 0 or new % XSV != 0)
+                inv_norm(it - 1, i)
+                before = (it - 1, i)
+            if new is not None and XEVI > 1:
+                rows_ev(new, XSV == 0 or new % XSV != 0)
+            if it in tab_at:
+                tab(*tab_at[it])
+        finish(*before)

@@ -20,7 +20,7 @@ GT = 2 * P
 NS = B * NPAIR
 NG = 2 * NS
 DUP = 0
-PLAIN = ()
+PLAIN = (4,)
 VFIRST = 1
 VSTEP = 2
 BMX = 3
@@ -34,7 +34,7 @@ HM = False
 NEG_G = True
 WEV = (False, True, True, True)
 XSV = 0
-SPIN_FIRST = 4
+SPIN_FIRST = 5
 HSPIN = 1
 FLOPS = 2 * B * T * D * 2 * DI
 

from contextlib import ExitStack

import concourse.mybir as mybir
from concourse.masks import make_identity

F32 = mybir.dt.float32
BF16 = mybir.dt.bfloat16
U32 = mybir.dt.uint32
U8 = mybir.dt.uint8
FP8X4 = mybir.dt.float8_e4m3fn_x4
ACT = mybir.ActivationFunctionType
ALU = mybir.AluOpType

P = 128
B, T, D, DI = 4, 1024, 512, 512
NT = T // P
NPAIR = NT // 2
NJ = DI // P
GT = 2 * P
NS = B * NPAIR
NG = 2 * NS
DUP = 0
PLAIN = (4,)
VFIRST = 1
VSTEP = 2
BMX = 3
BR = 5
TLEAD = 6
TSTEP = 2
XFIRST = True
XEVI = 0
HQ = True
HM = False
NEG_G = True
WEV = (False, True, True, True)
XSV = 0
SPIN_FIRST = 5
HSPIN = 1
FLOPS = 2 * B * T * D * 2 * DI


def tile_attentionhead_pa_t_kernel(tc, input_vecs, qk_w, sqk, cos, sin, out_0, out_1):
    nc = tc.nc
    x_v = input_vecs.rearrange("b (p n) k -> b p n k", n=NT)
    w_v = qk_w.rearrange("(h t r p) k -> p h r t k", p=P, r=2, t=2)
    cos_v = cos.rearrange("(p n) c -> p n c", n=NT)
    sin_v = sin.rearrange("(p n) c -> p n c", n=NT)
    o_v = [o.rearrange("b (p n) c -> b p n c", n=NT) for o in (out_0, out_1)]

    with ExitStack() as ctx:
        const = ctx.enter_context(tc.tile_pool(name="const", bufs=1))
        stage = ctx.enter_context(tc.tile_pool(name="stage", bufs=3))
        prods = ctx.enter_context(tc.tile_pool(name="prods", bufs=6))
        outs = ctx.enter_context(tc.tile_pool(name="outs", bufs=6))
        small = ctx.enter_context(tc.tile_pool(name="small", bufs=6))
        psum_mx = ctx.enter_context(tc.psum_pool(name="psum_mx", bufs=BMX))
        psum_tp = ctx.enter_context(tc.psum_pool(name="psum_tp", bufs=BR))
        ctx.enter_context(tc.manual_schedule())

        xr = const.tile([P, NS, 2, D], BF16, name="xr")
        wr = const.tile([P, 2, 2, 2, D], BF16, name="wr")
        cr = const.tile([P, NT, DI], BF16, name="cr")
        sr = const.tile([P, NT, DI], BF16, name="sr")
        gb = const.tile([P, DI], BF16, name="gb")
        xc = const.tile([P, B * T], U32, name="xc", align_bytes=64)
        xs = const.tile([P, B * T], U8, name="xs", align_bytes=64)
        wc = const.tile([P, 2 * DI], U32, name="wc", align_bytes=64)
        ws = const.tile([P, 2 * DI], U8, name="ws", align_bytes=64)
        tabs = const.tile([P, NPAIR, 2, 2, 2, GT], BF16, name="tabs")

        def load_w(h, pr):
            nc.sync.dma_start(out=wr[:, h, pr], in_=w_v[:, h, pr])

        def load_x(n):
            q, b = divmod(n, B)
            nc.sync.dma_start(out=xr[:, n], in_=x_v[b][:, 2 * q : 2 * q + 2, :])

        def load_tab(q):
            pair = slice(2 * q, 2 * q + 2)
            nc.sync.dma_start(out=cr[:, pair, :], in_=cos_v[:, pair, :])
            nc.sync.dma_start(out=sr[:, pair, :], in_=sin_v[:, pair, :])

        load_w(0, 0)
        load_x(0)
        load_tab(0)
        load_w(0, 1)
        load_w(1, 0)
        load_w(1, 1)
        load_x(1)
        nc.sync.dma_start(out=gb[:], in_=sqk.partition_broadcast(P))
        for n in range(2, NS):
            load_x(n)
            if n % B == 2 and n // B + 1 < NPAIR:
                load_tab(n // B + 1)

        zl = const.tile([P, P], BF16, name="zl")
        nc.vector.memset(zl[:], 0.0)
        zr = const.tile([P, 2 * GT], BF16, name="zr")
        nc.vector.memset(zr[:], 0.0)
        ident_f = const.tile([P, P], F32, name="ident_f")
        make_identity(nc, ident_f[:])
        ident_b = const.tile([P, P], BF16, name="ident_b")
        make_identity(nc, ident_b[:])
        one = const.tile([P, 1], F32, name="one")
        nc.vector.memset(one[:], 1.0)
        warm = const.tile([P, 1], F32, name="warm")
        nc.scalar.activation(out=warm[:], in_=one[:], func=ACT.Abs_reciprocal_sqrt)
        dm = psum_mx.tile([P, 2 * GT], F32, tag="mx", name="dm")

        def spin(n):
            for rep in range(n):
                nc.tensor.matmul(out=dm[:], lhsT=zl[:], rhs=zr[:], start=True, stop=True)

        spin(SPIN_FIRST)

        grouped = {}
        word_banks = {}
        banks = {}
        prod_tiles = {}
        r_banks = {}
        norm_tiles = {}

        def rows_tp(key, rows):
            pt = psum_tp.tile([P, 2, 2, P], F32, tag="tp", name="pt")
            word_banks[key] = pt
            for i in range(2):
                words = rows[i].bitcast(F32)
                for u in range(2):
                    nc.tensor.transpose(pt[:, i, u, :], words[:, u : D // 2 : 2], ident_f[:])

        def rows_ev(key, on_scalar):
            g_t = stage.tile([P, 2 * P * 4], BF16, tag="g", name="g_t", align_bytes=64)
            grouped[key] = g_t
            gw = g_t[:].bitcast(F32).rearrange("p (i r u) -> p i r u", i=2, u=2)
            src = word_banks[key][:].rearrange("p i u r -> p i r u")
            if on_scalar:
                nc.scalar.copy(out=gw, in_=src)
            else:
                nc.vector.tensor_copy(out=gw, in_=src)

        def w_tp(h, pr):
            rows_tp(("w", h, pr), [wr[:, h, pr, t, :] for t in range(2)])

        def w_ev(h, pr):
            rows_ev(("w", h, pr), WEV[2 * h + pr])

        def w_q(h, pr):
            cols = slice((2 * h + pr) * GT, (2 * h + pr + 1) * GT)
            nc.vector.quantize_mx(out=wc[:, cols].bitcast(FP8X4), scales=ws[:, cols], in_=grouped[("w", h, pr)][:])

        def x_tp(n):
            rows_tp(n, [xr[:, n, i, :] for i in range(2)])

        def x_q(n):
            cols = slice(n * GT, (n + 1) * GT)
            nc.vector.quantize_mx(out=xc[:, cols].bitcast(FP8X4), scales=xs[:, cols], in_=grouped[n][:])

        def tab(q, pr):
            ptb = psum_tp.tile([P, 4, GT], BF16, tag="tp", name="ptb")
            for n, (raw, j) in enumerate(((cr, pr), (cr, pr + 2), (sr, pr + 2), (sr, pr))):
                for i in range(2):
                    nc.tensor.transpose(
                        ptb[:, n, i * P : (i + 1) * P], raw[:, 2 * q + i, j * P : (j + 1) * P], ident_b[:]
                    )
            out = tabs[:, q, pr].rearrange("p c t r -> p (c t) r")
            if q == 0 or not NEG_G:
                nc.scalar.copy(out=out[:, 0:3], in_=ptb[:, 0:3])
                nc.scalar.mul(out=out[:, 3], in_=ptb[:, 3], mul=-1.0)
            else:
                nc.scalar.copy(out=out, in_=ptb[:])

        def negate(q):
            half = sr[:, 2 * q : 2 * q + 2, 0 : DI // 2]
            nc.gpsimd.tensor_scalar(out=half, in0=half, scalar1=-1.0, scalar2=0.0, op0=ALU.mult, op1=ALU.add)

        def mx(g, pr):
            n, h = divmod(g, 2)
            tok = slice(n * GT, (n + 1) * GT)
            x2 = psum_mx.tile([P, 2, GT], F32, tag="mx", name="x2")
            banks[(g, pr)] = x2
            for t in range(2):
                c0 = ((2 * h + pr) * 2 + t) * P
                for rep in range(2 if 2 * pr + t < DUP and g > 0 else 1):
                    nc.tensor.matmul_mx(
                        out=x2[:, t, :],
                        lhsT=wc[:, c0 : c0 + P].bitcast(FP8X4),
                        lhsT_scale=ws[:, c0 : c0 + P],
                        rhs=xc[:, tok].bitcast(FP8X4),
                        rhs_scale=xs[:, tok],
                        start=True,
                        stop=True,
                    )

        def prod(g, pr, ts=slice(0, GT)):
            q = g // (2 * B)
            if ts.start == 0:
                prod_tiles[(g, pr)] = prods.tile([P, 2, 2, GT], F32, tag="ab", name="ab")
            nc.vector.tensor_tensor(
                out=prod_tiles[(g, pr)][:, :, :, ts],
                in0=banks[(g, pr)][:, :, ts].unsqueeze(1).to_broadcast([P, 2, 2, ts.stop - ts.start]),
                in1=tabs[:, q, pr, :, :, ts],
                op=ALU.mult,
            )

        def add_t(g):
            r_banks[g] = []
            for i in range(2):
                rb = psum_tp.tile([P, DI], F32, tag="tp", name="rb")
                r_banks[g].append(rb)
                ts = slice(i * P, (i + 1) * P)
                for pr in range(2):
                    ab = prod_tiles[(g, pr)]
                    for t in range(2):
                        j = pr + 2 * t
                        cs = slice(j * P, (j + 1) * P)
                        nc.tensor.matmul(
                            out=rb[:, cs],
                            lhsT=ab[:, 0, t, ts],
                            rhs=ident_f[:],
                            is_transpose=4 * i + 2 * pr + t not in PLAIN,
                            start=True,
                            stop=False,
                        )
                        nc.tensor.matmul(
                            out=rb[:, cs],
                            lhsT=ab[:, 1, 1 - t, ts],
                            rhs=ident_f[:],
                            is_transpose=True,
                            start=False,
                            stop=True,
                        )

        def sum_squares(g, i):
            if i == 0:
                ssq = small.tile([P, 2], F32, tag="ssq", name="ssq")
                rho = small.tile([P, 2], F32, tag="rho", name="rho")
                ot = outs.tile([P, 2, DI], F32, tag="ot", name="ot")
                norm_tiles[g] = (ssq, rho, ot)
            junk = stage.tile([P, DI], BF16, tag="junk", name="junk")
            nc.scalar.activation(
                out=junk[:], in_=r_banks[g][i][:], func=ACT.Square, accum_out=norm_tiles[g][0][:, i : i + 1]
            )

        def inv_norm(g, i):
            ssq, rho, ot = norm_tiles[g]
            col = slice(i, i + 1)
            nc.scalar.activation(out=rho[:, col], in_=ssq[:, col], func=ACT.Abs_reciprocal_sqrt, scale=1.0 / D)

        def scale_out(g, i):
            ssq, rho, ot = norm_tiles[g]
            nc.scalar.activation(out=ot[:, i, :], in_=r_banks[g][i][:], func=ACT.Copy, scale=rho[:, i : i + 1])

        def norm_gain_on_v(g, i):
            ssq, rho, ot = norm_tiles[g]
            nc.vector.scalar_tensor_tensor(
                out=ot[:, i, :],
                in0=r_banks[g][i][:],
                scalar=rho[:, i : i + 1],
                in1=gb[:],
                op0=ALU.mult,
                op1=ALU.mult,
            )

        def gain(g, lo, hi):
            ot = norm_tiles[g][2]
            nc.gpsimd.tensor_tensor(
                out=ot[:, lo:hi, :],
                in0=ot[:, lo:hi, :],
                in1=gb[:].unsqueeze(1).to_broadcast([P, hi - lo, DI]),
                op=ALU.mult,
            )

        def store(g, lo, hi):
            n, h = divmod(g, 2)
            q, b = divmod(n, B)
            nc.sync.dma_start(out=o_v[h][b][:, 2 * q + lo : 2 * q + hi, :], in_=norm_tiles[g][2][:, lo:hi, :])

        def on_v(g):
            return g >= VFIRST and (g - VFIRST) % VSTEP == 0

        last = NG - 1

        def finish(g, i):
            if g == last or (g == last - 1 and i == 1):
                norm_gain_on_v(g, i)
                store(g, i, i + 1)
            elif g == last - 1:
                scale_out(g, i)
                gain(g, i, i + 1)
                store(g, i, i + 1)
            elif i == 0 or not on_v(g):
                scale_out(g, i)
                if i == 1 or on_v(g):
                    gain(g, 0, i + 1)
                    store(g, 0, i + 1)

        w_tp(0, 0)
        w_ev(0, 0)
        x_tp(0)
        rows_ev(0, False)
        tab(0, 0)
        w_q(0, 0)
        x_q(0)
        spin(HSPIN)
        if HM:
            mx(0, 0)
        w_tp(0, 1)
        w_ev(0, 1)
        if not HM:
            mx(0, 0)
        tab(0, 1)
        if HQ:
            w_q(0, 1)
        prod(0, 0)
        if not HQ:
            w_q(0, 1)
        spin(HSPIN)
        w_tp(1, 0)
        w_ev(1, 0)
        mx(0, 1)
        w_tp(1, 1)
        w_ev(1, 1)
        w_q(1, 0)
        prod(0, 1)
        x_tp(1)
        rows_ev(1, True)
        mx(1, 0)
        w_q(1, 1)
        x_q(1)
        mx(1, 1)
        for q in range(1, NPAIR):
            if NEG_G:
                negate(q)

        tab_at = {}
        for q in range(1, NPAIR):
            for pr in range(2):
                tab_at[2 * B * q - TLEAD + TSTEP * pr] = (q, pr)
        before = None
        for it in range(1, NG + 1):
            new = (it + 3) // 2 if it % 2 == 1 and (it + 3) // 2 < NS else None
            if new is not None and XFIRST:
                x_tp(new)
            add_t(it - 1)
            if new is not None and not XFIRST:
                x_tp(new)
            if it == last:
                for half in range(2):
                    for pr in range(2):
                        prod(it, pr, slice(half * P, (half + 1) * P))
            elif it < last:
                prod(it, 0)
                prod(it, 1)
            if it % 2 == 0 and (it + 2) // 2 < NS:
                x_q((it + 2) // 2)
            if it >= 2 and it - 2 < last - 1 and on_v(it - 2):
                norm_gain_on_v(it - 2, 1)
                store(it - 2, 1, 2)
            if it + 1 < NG:
                mx(it + 1, 0)
                mx(it + 1, 1)
            for i in range(2):
                sum_squares(it - 1, i)
                if before is not None:
                    finish(*before)
                if new is not None and i == XEVI:
                    rows_ev(new, XSV == 0 or new % XSV != 0)
                inv_norm(it - 1, i)
                before = (it - 1, i)
            if new is not None and XEVI > 1:
                rows_ev(new, XSV == 0 or new % XSV != 0)
            if it in tab_at:
                tab(*tab_at[it])
        finish(*before)
